import numpy as np
import ml_dtypes


def mxq(x, axis, fmt="e4m3"):
    dtype, down = {"e4m3": (ml_dtypes.float8_e4m3fn, 7), "e5m2": (ml_dtypes.float8_e5m2, 14)}[fmt]
    v = np.moveaxis(np.asarray(x, np.float32).astype(ml_dtypes.bfloat16).astype(np.float64), axis, -1)
    blocks = v.reshape(v.shape[:-1] + (-1, 32))
    amax = np.abs(blocks).max(-1, keepdims=True)
    byte = np.maximum(np.where(amax > 0, np.frexp(amax)[1] - 1 + 127, 0) - down, 1)
    scale = np.exp2(byte - 127.0)
    codes = (blocks / scale).astype(np.float32).astype(dtype).astype(np.float64)
    return np.moveaxis((codes * scale).reshape(v.shape), -1, axis)


WIDE = False


def mx_kscale(k):
    if not WIDE:
        return np.ones(k)
    levels = np.array([10, -10, 5, -5, 0])
    if k % 512:
        return np.exp2(np.random.permutation(np.resize(levels, k // 32))).repeat(32)
    a = np.empty((k // 512, 16))
    for p in range(k // 512):
        a[p, :8] = np.random.permutation(np.resize(levels, 8))
        for g in range(8):
            far = levels[np.abs(levels - a[p, g]) >= 10]
            a[p, g + 8] = far[np.random.randint(len(far))]
    return np.exp2(a.ravel()).repeat(32)


BF16 = ml_dtypes.bfloat16


def bf(x):
    return np.asarray(x, np.float32).astype(BF16)


def f64(x):
    return np.asarray(x).astype(np.float64)


N, M, E, F, Z = 4, 1536, 2048, 1024, 256


def embed(xq, w1q, b1, w2q, b2):
    h = np.maximum((xq @ w1q) + b1, 0.0)
    return np.maximum((mxq(h, 2, "e4m3") @ w2q) + b2, 0.0)


def setup_inputs():
    s, t = mx_kscale(E), mx_kscale(F)
    return {"xp1": bf(np.random.standard_normal((N, M, E)) * s),
            "xp2": bf(np.random.standard_normal((N, M, E)) * s),
            "W1": bf(np.random.standard_normal((E, F)) / np.sqrt(E) / s[:, None] * t),
            "b1": bf(np.random.standard_normal(F) * 0.3 * t),
            "W2": bf(np.random.standard_normal((F, Z)) * 2.0 / np.sqrt(F) / t[:, None]),
            "b2": bf(np.random.standard_normal(Z) * 0.3),
            "q_energy": bf(1.0 + 0.25 * np.random.standard_normal((N, M)))}


def reference(xp1, xp2, W1, b1, W2, b2, q_energy):
    w1q = mxq(f64(W1), 0, "e4m3")
    w2q = mxq(f64(W2), 0, "e4m3")
    z1 = embed(mxq(f64(xp1), 2, "e4m3"), w1q, f64(b1), w2q, f64(b2))
    z2 = embed(mxq(f64(xp2), 2, "e4m3"), w1q, f64(b1), w2q, f64(b2))
    d = z1 - z2
    return f64(q_energy) * np.mean(d * d, axis=2)

@@ -1,0 +1,308 @@
+from contextlib import ExitStack
+
+import concourse.mybir as mybir
+from concourse.masks import make_identity
+
+F32 = mybir.dt.float32
+BF16 = mybir.dt.bfloat16
+U32 = mybir.dt.uint32
+U8 = mybir.dt.uint8
+FP8X4 = mybir.dt.float8_e4m3fn_x4
+ACT = mybir.ActivationFunctionType
+ALU = mybir.AluOpType
+
+P = 128
+E, F, Z = 2048, 1024, 256
+ROWS = 6144
+SUB = ROWS // P
+NCHUNK = 24
+NSTEP = 2 * NCHUNK
+FLOPS = 2 * 2 * ROWS * (E * F + F * Z)
+
+NRAW = 4
+XRAW_BUFS = 6
+
+
+def tile_querysiamese_pa_l_kernel(tc, xp1, xp2, W1, b1, W2, b2, q_energy, out):
+    nc = tc.nc
+    with ExitStack() as ctx:
+        ctx.enter_context(tc.manual_schedule())
+        keep = ctx.enter_context(tc.tile_pool(name="keep", bufs=1))
+        work = ctx.enter_context(tc.tile_pool(name="work", bufs=1))
+        psum = ctx.enter_context(tc.psum_pool(name="psum", bufs=1))
+
+        xv = [xp.rearrange("a (b s) k -> (a b) s k", s=SUB) for xp in (xp1, xp2)]
+
+        ident = keep.tile([P, P], F32, name="ident", tag="ident")
+        make_identity(nc, ident[:])
+        negones = keep.tile([P, P], BF16, name="negones", tag="negones")
+        nc.vector.memset(negones[:], -1.0)
+        brow = keep.tile([P, Z], BF16, name="brow", tag="brow")
+        nc.vector.memset(brow[:], 0.0)
+        warm = keep.tile([P, 1], F32, name="warm", tag="warm")
+        nc.vector.memset(warm[:], 0.0)
+        warm2 = keep.tile([P, 1], F32, name="warm2", tag="warm2")
+        nc.scalar.activation(out=warm2[:], in_=warm[:], func=ACT.Relu)
+
+        nc.sync.dma_start(out=brow[0:1, :], in_=b2.rearrange("(o z) -> o z", o=1))
+        b1t = keep.tile([P, 2, 4], BF16, name="b1t", tag="b1t")
+        nc.sync.dma_start(out=b1t[:], in_=b1.rearrange("(g p t) -> p g t", g=2, t=4))
+
+        w1q = keep.tile([P, 4, F], U32, name="w1q", tag="w1q", align_bytes=64)
+        w1s = keep.tile([P, 4, F], U8, name="w1s", tag="w1s", align_bytes=64)
+        w2q = keep.tile([P, 2 * Z], U32, name="w2q", tag="w2q", align_bytes=64)
+        w2s = keep.tile([P, 2 * Z], U8, name="w2s", tag="w2s", align_bytes=64)
+        nb2 = keep.tile([P, 2, Z], F32, name="nb2", tag="nb2")
+        b1f = keep.tile([P, 8], F32, name="b1f", tag="b1f")
+        res = keep.tile([P, SUB], F32, name="res", tag="res")
+        qt = keep.tile([P, SUB], BF16, name="qt", tag="qt")
+
+        xraw = {}
+        xs = {}
+        xg = {}
+        xq = {}
+        xsc = {}
+        ps1 = {}
+        hT = {}
+        hg = {}
+        hq = {}
+        hsc = {}
+        ps2 = {}
+        mt = {}
+        dt_ = {}
+        w1raw = {}
+        w1g = {}
+        state = {"next_load": XRAW_BUFS}
+
+        def load(rho):
+            chunk, gp = rho // 2, rho % 2
+            tower, j = chunk % 2, chunk // 2
+            t = work.tile([P, 4, 1024], BF16, name="xraw", tag="xraw", bufs=XRAW_BUFS)
+            nc.sync.dma_start(out=t[:], in_=xv[tower][:, 4 * j:4 * j + 4, 1024 * gp:1024 * gp + 1024])
+            xraw[rho] = t
+
+        def raw_words(rho):
+            return xraw[rho][:].bitcast(F32).rearrange("p r (g m u) -> p r g m u", g=2, u=2)
+
+        def sort(rho):
+            words = raw_words(rho)
+            for g2 in range(2):
+                s = work.tile([P, 4, 2, P], F32, name="xs", tag="xs", bufs=4)
+                nc.vector.tensor_copy(out=s[:], in_=words[:, :, g2].rearrange("p r m u -> p r u m"))
+                xs[(rho, g2)] = s
+            xraw.pop(rho)
+
+        def trun(rho):
+            for g2 in range(2):
+                grouped = work.tile([P, 512, 4], BF16, name="xg", tag="xg", bufs=4, align_bytes=64)
+                xg[(rho, g2)] = grouped
+                gw = grouped[:].rearrange("p n t -> p (n t)").bitcast(F32).rearrange(
+                    "p (r n u) -> p r n u", r=4, u=2)
+                for rp in range(2):
+                    tp = psum.tile([P, 2, 2, P], F32, name="tp", tag="tp", bufs=4)
+                    for r2 in range(2):
+                        for u in range(2):
+                            if rho < NRAW:
+                                src = raw_words(rho)[:, 2 * rp + r2, g2, :, u]
+                            else:
+                                src = xs[(rho, g2)][:, 2 * rp + r2, u, :]
+                            nc.tensor.transpose(tp[:, r2, u, :], src, ident[:])
+                    nc.scalar.copy(out=gw[:, 2 * rp:2 * rp + 2], in_=tp[:].rearrange("p r u n -> p r n u"))
+                if rho >= NRAW:
+                    xs.pop((rho, g2))
+            if rho < NRAW:
+                xraw.pop(rho)
+
+        def qx(rho, g2):
+            chunk, gp = rho // 2, rho % 2
+            g = 2 * gp + g2
+            if g == 0:
+                xq[chunk] = work.tile([P, 4, 512], U32, name="xq", tag="xq", bufs=2, align_bytes=64)
+                xsc[chunk] = work.tile([P, 4, 512], U8, name="xsc", tag="xsc", bufs=2, align_bytes=64)
+            nc.vector.quantize_mx(
+                out=xq[chunk][:, g, :].bitcast(FP8X4),
+                scales=xsc[chunk][:, g, :],
+                in_=xg.pop((rho, g2))[:].rearrange("p n t -> p (n t)"),
+            )
+
+        def s1(tau, t):
+            chunk, G = tau // 2, tau % 2
+            c = 4 * G + t
+            acc = psum.tile([P, 512], F32, name="ps1", tag="ps1", bufs=3)
+            for g in range(4):
+                nc.tensor.matmul_mx(
+                    out=acc[:],
+                    lhsT=w1q[:, g, P * c:P * c + P].bitcast(FP8X4),
+                    lhsT_scale=w1s[:, g, P * c:P * c + P],
+                    rhs=xq[chunk][:, g, :].bitcast(FP8X4),
+                    rhs_scale=xsc[chunk][:, g, :],
+                    start=(g == 0),
+                    stop=(g == 3),
+                )
+            if t == 0:
+                hT[tau] = work.tile([P, 4, 512], BF16, name="hT", tag="hT", bufs=2)
+            nc.scalar.activation(out=hT[tau][:, t, :], in_=acc[:], func=ACT.Relu, bias=b1f[:, c:c + 1], scale=1.0)
+
+        def hint(tau):
+            hg[tau] = work.tile([P, 512, 4], BF16, name="hg", tag="hg", bufs=2, align_bytes=64)
+            nc.vector.tensor_copy(out=hg[tau][:], in_=hT.pop(tau)[:].rearrange("p t n -> p n t"))
+
+        def qh(tau):
+            chunk, G = tau // 2, tau % 2
+            if G == 0:
+                hq[chunk] = work.tile([P, 2, 512], U32, name="hq", tag="hq", bufs=2, align_bytes=64)
+                hsc[chunk] = work.tile([P, 2, 512], U8, name="hsc", tag="hsc", bufs=2, align_bytes=64)
+            nc.vector.quantize_mx(
+                out=hq[chunk][:, G, :].bitcast(FP8X4),
+                scales=hsc[chunk][:, G, :],
+                in_=hg.pop(tau)[:].rearrange("p n t -> p (n t)"),
+            )
+
+        def s2(sig):
+            chunk, rp = sig // 2, sig % 2
+            acc = psum.tile([P, 2, Z], F32, name="ps2", tag="ps2", bufs=1)
+            for r2 in range(2):
+                r = 2 * rp + r2
+                for G in range(2):
+                    nc.tensor.matmul_mx(
+                        out=acc[:, r2, :],
+                        lhsT=hq[chunk][:, G, P * r:P * r + P].bitcast(FP8X4),
+                        lhsT_scale=hsc[chunk][:, G, P * r:P * r + P],
+                        rhs=w2q[:, Z * G:Z * G + Z].bitcast(FP8X4),
+                        rhs_scale=w2s[:, Z * G:Z * G + Z],
+                        start=(G == 0),
+                        stop=(G == 1),
+                    )
+            ps2[sig] = acc
+
+        def maxb(sig):
+            mt[sig] = work.tile([P, 2, Z], F32, name="mt", tag="mt", bufs=4)
+            nc.vector.tensor_tensor(out=mt[sig][:], in0=ps2.pop(sig)[:], in1=nb2[:], op=ALU.max)
+
+        def diff(sig):
+            dt_[sig] = work.tile([P, 2, Z], F32, name="dd", tag="dd", bufs=2)
+            nc.vector.tensor_tensor(out=dt_[sig][:], in0=mt.pop(sig - 2)[:], in1=mt.pop(sig)[:], op=ALU.subtract)
+
+        def sq(sig):
+            chunk, rp = sig // 2, sig % 2
+            j = chunk // 2
+            d = dt_.pop(sig)
+            for r2 in range(2):
+                s = 4 * j + 2 * rp + r2
+                junk = work.tile([P, Z], F32, name="junk", tag="junk", bufs=2)
+                nc.scalar.activation(out=junk[:], in_=d[:, r2, :], func=ACT.Square, scale=1.0 / 16.0,
+                                     accum_out=res[:, s:s + 1])
+
+        def w1_load(G, g):
+            t = work.tile([P, 4, 512], BF16, name="w1raw", tag="w1raw", bufs=4)
+            nc.sync.dma_start(
+                out=t[:],
+                in_=W1[512 * g:512 * g + 512, 512 * G:512 * G + 512].rearrange("(p j) c -> p j c", j=4))
+            w1raw[(G, g)] = t
+
+        def w1_copy(G, g, eng):
+            t = work.tile([P, 2048], BF16, name="w1g", tag="w1g", bufs=3, align_bytes=64)
+            dst = t[:].rearrange("p (t m j) -> p t m j", t=4, j=4)
+            src = w1raw.pop((G, g))[:].rearrange("p j (m t) -> p t m j", t=4)
+            if eng == 0:
+                nc.vector.tensor_copy(out=dst, in_=src)
+            else:
+                nc.scalar.copy(out=dst, in_=src)
+            w1g[(G, g)] = t
+
+        def w1_quant(G, g):
+            nc.vector.quantize_mx(
+                out=w1q[:, g, 512 * G:512 * G + 512].bitcast(FP8X4),
+                scales=w1s[:, g, 512 * G:512 * G + 512],
+                in_=w1g.pop((G, g))[:],
+            )
+
+        def step(tau):
+            sig = tau - 3
+            live = 0 <= tau < NSTEP
+            second = 0 <= sig < NSTEP and (sig // 2) % 2 == 1
+            if 0 <= sig < NSTEP:
+                maxb(sig)
+            if live:
+                s1(tau, 0)
+                s1(tau, 1)
+            if 0 <= tau - 1 < NSTEP:
+                hint(tau - 1)
+            if second:
+                diff(sig)
+            if 0 <= tau + 2 < NSTEP:
+                trun(tau + 2)
+            if NRAW <= tau + 3 < NSTEP:
+                sort(tau + 3)
+            if 0 <= tau - 1 < NSTEP:
+                qh(tau - 1)
+            if 0 <= tau + 2 < NSTEP:
+                qx(tau + 2, 0)
+            if live:
+                s1(tau, 2)
+            if second:
+                sq(sig)
+            if live:
+                s1(tau, 3)
+            if 0 <= tau + 2 < NSTEP:
+                qx(tau + 2, 1)
+            if 0 <= tau - 2 < NSTEP:
+                s2(tau - 2)
+            while tau >= 0 and state["next_load"] < min(tau + XRAW_BUFS + 3, NSTEP):
+                load(state["next_load"])
+                state["next_load"] = state["next_load"] + 1
+
+        load(0)
+        load(1)
+        for g in range(4):
+            w1_load(0, g)
+        load(2)
+
+        psb = psum.tile([P, 2, Z], F32, name="ps2", tag="ps2", bufs=1)
+        for r2 in range(2):
+            nc.tensor.matmul(out=psb[:, r2, :], lhsT=negones[:], rhs=brow[:], start=True, stop=True)
+        nc.vector.tensor_copy(out=nb2[:], in_=psb[:])
+        nc.vector.tensor_copy(out=b1f[:], in_=b1t[:].rearrange("p g t -> p (g t)"))
+
+        step(-2)
+        w1_copy(0, 0, 0)
+        step(-1)
+        w1_copy(0, 1, 1)
+        w1_quant(0, 0)
+        w1_copy(0, 2, 0)
+        w1_copy(0, 3, 0)
+        w1_quant(0, 1)
+        w1_quant(0, 2)
+        w1_quant(0, 3)
+
+        for g in range(4):
+            w1_load(1, g)
+        load(3)
+        load(4)
+        load(5)
+
+        w1_copy(1, 0, 1)
+        w1_copy(1, 1, 0)
+        w1_quant(1, 0)
+        w1_copy(1, 2, 0)
+        w1_quant(1, 1)
+        w1_copy(1, 3, 0)
+        w1_quant(1, 2)
+        w1_quant(1, 3)
+
+        w2raw = work.tile([P, 2, 4, Z], BF16, name="w1raw", tag="w1raw", bufs=4)
+        nc.sync.dma_start(out=w2raw[:], in_=W2.rearrange("(g p j) z -> p g j z", g=2, j=4))
+        nc.sync.dma_start(out=qt[:], in_=q_energy.rearrange("a (b s) -> (a b) s", s=SUB))
+
+        step(0)
+        step(1)
+        w2g = work.tile([P, 2, Z, 4], BF16, name="w1g", tag="w1g", bufs=3, align_bytes=64)
+        nc.vector.tensor_copy(out=w2g[:], in_=w2raw[:].rearrange("p g j z -> p g z j"))
+        nc.vector.quantize_mx(out=w2q[:].bitcast(FP8X4), scales=w2s[:],
+                              in_=w2g[:].rearrange("p g z j -> p (g z j)"))
+        for tau in range(2, NSTEP + 3):
+            step(tau)
+
+        o = keep.tile([P, SUB], F32, name="o", tag="o")
+        nc.vector.tensor_tensor(out=o[:], in0=res[:], in1=qt[:], op=ALU.mult)
+        nc.sync.dma_start(out=out.rearrange("a (b s) -> (a b) s", s=SUB), in_=o[:])

@@ -73,6 +73,7 @@ def tile_querysiamese_pa_l_kernel(tc, xp1, xp2, W1, b1, W2, b2, q_energy, out):
         w1raw = {}
         w1g = {}
         state = {"next_load": XRAW_BUFS}
+        hacc = {}
 
         def load(rho):
             chunk, gp = rho // 2, rho % 2
@@ -125,42 +126,66 @@ def tile_querysiamese_pa_l_kernel(tc, xp1, xp2, W1, b1, W2, b2, q_energy, out):
                 in_=xg.pop((rho, g2))[:].rearrange("p n t -> p (n t)"),
             )
 
-        def s1(tau, t):
+        def mm1(acc, tau, t, g):
             chunk, G = tau // 2, tau % 2
             c = 4 * G + t
-            acc = psum.tile([P, 512], F32, name="ps1", tag="ps1", bufs=3)
-            for g in range(4):
-                nc.tensor.matmul_mx(
-                    out=acc[:],
-                    lhsT=w1q[:, g, P * c:P * c + P].bitcast(FP8X4),
-                    lhsT_scale=w1s[:, g, P * c:P * c + P],
-                    rhs=xq[chunk][:, g, :].bitcast(FP8X4),
-                    rhs_scale=xsc[chunk][:, g, :],
-                    start=(g == 0),
-                    stop=(g == 3),
-                )
+            nc.tensor.matmul_mx(
+                out=acc[:],
+                lhsT=w1q[:, g, P * c:P * c + P].bitcast(FP8X4),
+                lhsT_scale=w1s[:, g, P * c:P * c + P],
+                rhs=xq[chunk][:, g, :].bitcast(FP8X4),
+                rhs_scale=xsc[chunk][:, g, :],
+                start=(g == 0),
+                stop=(g == 3),
+            )
+
+        def hout(acc, tau, t):
+            c = 4 * (tau % 2) + t
             if t == 0:
                 hT[tau] = work.tile([P, 4, 512], BF16, name="hT", tag="hT", bufs=2)
             nc.scalar.activation(out=hT[tau][:, t, :], in_=acc[:], func=ACT.Relu, bias=b1f[:, c:c + 1], scale=1.0)
 
-        def hint(tau):
-            hg[tau] = work.tile([P, 512, 4], BF16, name="hg", tag="hg", bufs=2, align_bytes=64)
-            nc.vector.tensor_copy(out=hg[tau][:], in_=hT.pop(tau)[:].rearrange("p t n -> p n t"))
+        def s1(tau, t):
+            acc = psum.tile([P, 512], F32, name="ps1", tag="ps1", bufs=3)
+            for g in range(4):
+                mm1(acc, tau, t, g)
+            hout(acc, tau, t)
 
-        def qh(tau):
+        def head_open(tau):
+            for t in range(3):
+                hacc[(tau, t)] = psum.tile([P, 512], F32, name="ps1", tag="ps1", bufs=3)
+            hacc[(tau, 3)] = psum.tile([P, 512], F32, name="ps2", tag="ps2", bufs=1)
+
+        def head_pass(tau, g):
+            for t in range(4):
+                mm1(hacc[(tau, t)], tau, t, g)
+
+        def head_close(tau):
+            for t in range(4):
+                hout(hacc.pop((tau, t)), tau, t)
+
+        def hint(tau, lo=0, hi=512):
+            if lo == 0:
+                hg[tau] = work.tile([P, 512, 4], BF16, name="hg", tag="hg", bufs=2, align_bytes=64)
+            nc.vector.tensor_copy(out=hg[tau][:, lo:hi, :], in_=hT[tau][:, :, lo:hi].rearrange("p t n -> p n t"))
+
+        def qh(tau, lo=0, hi=512):
             chunk, G = tau // 2, tau % 2
-            if G == 0:
+            if G == 0 and lo == 0:
                 hq[chunk] = work.tile([P, 2, 512], U32, name="hq", tag="hq", bufs=2, align_bytes=64)
                 hsc[chunk] = work.tile([P, 2, 512], U8, name="hsc", tag="hsc", bufs=2, align_bytes=64)
             nc.vector.quantize_mx(
-                out=hq[chunk][:, G, :].bitcast(FP8X4),
-                scales=hsc[chunk][:, G, :],
-                in_=hg.pop(tau)[:].rearrange("p n t -> p (n t)"),
+                out=hq[chunk][:, G, lo:hi].bitcast(FP8X4),
+                scales=hsc[chunk][:, G, lo:hi],
+                in_=hg[tau][:, lo:hi, :].rearrange("p n t -> p (n t)"),
             )
 
-        def s2(sig):
+        def s2(sig, spare=False):
             chunk, rp = sig // 2, sig % 2
-            acc = psum.tile([P, 2, Z], F32, name="ps2", tag="ps2", bufs=1)
+            if spare:
+                acc = psum.tile([P, 2, Z], F32, name="tp", tag="tp", bufs=4)
+            else:
+                acc = psum.tile([P, 2, Z], F32, name="ps2", tag="ps2", bufs=1)
             for r2 in range(2):
                 r = 2 * rp + r2
                 for G in range(2):
@@ -194,7 +219,7 @@ def tile_querysiamese_pa_l_kernel(tc, xp1, xp2, W1, b1, W2, b2, q_energy, out):
                                      accum_out=res[:, s:s + 1])
 
         def w1_load(G, g):
-            t = work.tile([P, 4, 512], BF16, name="w1raw", tag="w1raw", bufs=4)
+            t = work.tile([P, 4, 512], BF16, name="w1raw", tag="w1raw", bufs=8)
             nc.sync.dma_start(
                 out=t[:],
                 in_=W1[512 * g:512 * g + 512, 512 * G:512 * G + 512].rearrange("(p j) c -> p j c", j=4))
@@ -253,10 +278,15 @@ def tile_querysiamese_pa_l_kernel(tc, xp1, xp2, W1, b1, W2, b2, q_energy, out):
                 state["next_load"] = state["next_load"] + 1
 
         load(0)
+        w1_load(0, 0)
+        w1_load(0, 1)
         load(1)
+        w1_load(0, 2)
+        w1_load(0, 3)
         for g in range(4):
-            w1_load(0, g)
-        load(2)
+            w1_load(1, g)
+        for rho in range(2, XRAW_BUFS):
+            load(rho)
 
         psb = psum.tile([P, 2, Z], F32, name="ps2", tag="ps2", bufs=1)
         for r2 in range(2):
@@ -264,44 +294,75 @@ def tile_querysiamese_pa_l_kernel(tc, xp1, xp2, W1, b1, W2, b2, q_energy, out):
         nc.vector.tensor_copy(out=nb2[:], in_=psb[:])
         nc.vector.tensor_copy(out=b1f[:], in_=b1t[:].rearrange("p g t -> p (g t)"))
 
-        step(-2)
+        trun(0)
         w1_copy(0, 0, 0)
-        step(-1)
-        w1_copy(0, 1, 1)
+        qx(0, 0)
         w1_quant(0, 0)
-        w1_copy(0, 2, 0)
-        w1_copy(0, 3, 0)
+        qx(0, 1)
+        w1_copy(0, 1, 1)
+        head_open(0)
+        head_pass(0, 0)
+        trun(1)
         w1_quant(0, 1)
+        head_pass(0, 1)
+        w1_copy(0, 2, 0)
+        qx(1, 0)
         w1_quant(0, 2)
+        head_pass(0, 2)
+        w1_copy(0, 3, 1)
+        qx(1, 1)
+        w1_copy(1, 0, 0)
         w1_quant(0, 3)
-
-        for g in range(4):
-            w1_load(1, g)
-        load(3)
-        load(4)
-        load(5)
-
-        w1_copy(1, 0, 1)
-        w1_copy(1, 1, 0)
-        w1_quant(1, 0)
-        w1_copy(1, 2, 0)
-        w1_quant(1, 1)
-        w1_copy(1, 3, 0)
-        w1_quant(1, 2)
-        w1_quant(1, 3)
-
-        w2raw = work.tile([P, 2, 4, Z], BF16, name="w1raw", tag="w1raw", bufs=4)
+        head_pass(0, 3)
+        w1_copy(1, 1, 1)
+        head_close(0)
+        w2raw = work.tile([P, 2, 4, Z], BF16, name="w1raw", tag="w1raw", bufs=8)
         nc.sync.dma_start(out=w2raw[:], in_=W2.rearrange("(g p j) z -> p g j z", g=2, j=4))
         nc.sync.dma_start(out=qt[:], in_=q_energy.rearrange("a (b s) -> (a b) s", s=SUB))
 
-        step(0)
-        step(1)
+        w1_copy(1, 2, 0)
+        w1_quant(1, 0)
+        w1_quant(1, 1)
+        head_open(1)
+        head_pass(1, 0)
+        head_pass(1, 1)
+        w1_copy(1, 3, 0)
+        w1_quant(1, 2)
+        trun(2)
+        head_pass(1, 2)
+        w1_quant(1, 3)
+        qx(2, 0)
+        qx(2, 1)
+        trun(3)
+        head_pass(1, 3)
+        head_close(1)
+        sort(4)
+        qx(3, 0)
+        qx(3, 1)
+        hint(0)
         w2g = work.tile([P, 2, Z, 4], BF16, name="w1g", tag="w1g", bufs=3, align_bytes=64)
         nc.vector.tensor_copy(out=w2g[:], in_=w2raw[:].rearrange("p g j z -> p g z j"))
+        qh(0)
         nc.vector.quantize_mx(out=w2q[:].bitcast(FP8X4), scales=w2s[:],
                               in_=w2g[:].rearrange("p g z j -> p (g z j)"))
-        for tau in range(2, NSTEP + 3):
+
+        for tau in range(2, NSTEP):
             step(tau)
+
+        last = NSTEP - 1
+        maxb(last - 2)
+        hint(last, 0, 256)
+        hint(last, 256, 512)
+        qh(last, 0, 256)
+        qh(last, 256, 512)
+        s2(last - 1)
+        s2(last, True)
+        maxb(last - 1)
+        maxb(last)
+        diff(last - 1)
+        diff(last)
+        sq(last - 1)
+        sq(last)
 
         o = keep.tile([P, SUB], F32, name="o", tag="o")
         nc.vector.tensor_tensor(out=o[:], in0=res[:], in1=qt[:], op=ALU.mult)

@@ -16,10 +16,9 @@ E, F, Z = 2048, 1024, 256
 ROWS = 6144
 SUB = ROWS // P
 NCHUNK = 24
-NSTEP = 2 * NCHUNK
 FLOPS = 2 * 2 * ROWS * (E * F + F * Z)
 
-NRAW = 4
+RAW_CHUNKS = 2
 XRAW_BUFS = 6
 
 
@@ -32,6 +31,13 @@ def tile_querysiamese_pa_l_kernel(tc, xp1, xp2, W1, b1, W2, b2, q_energy, out):
         psum = ctx.enter_context(tc.psum_pool(name="psum", bufs=1))
 
         xv = [xp.rearrange("a (b s) k -> (a b) s k", s=SUB) for xp in (xp1, xp2)]
+        state = {"next_load": 0, "bank": 0}
+
+        def bank(shape, idx=None):
+            if idx is None:
+                idx = state["bank"] % 8
+                state["bank"] = state["bank"] + 1
+            return psum.tile(shape, F32, name="bank%d" % idx, tag="bank%d" % idx)
 
         ident = keep.tile([P, P], F32, name="ident", tag="ident")
         make_identity(nc, ident[:])
@@ -62,160 +68,143 @@ def tile_querysiamese_pa_l_kernel(tc, xp1, xp2, W1, b1, W2, b2, q_energy, out):
         xg = {}
         xq = {}
         xsc = {}
-        ps1 = {}
         hT = {}
         hg = {}
         hq = {}
         hsc = {}
         ps2 = {}
         mt = {}
-        dt_ = {}
+        dd = {}
         w1raw = {}
         w1g = {}
-        state = {"next_load": XRAW_BUFS}
         hacc = {}
 
-        def load(rho):
-            chunk, gp = rho // 2, rho % 2
-            tower, j = chunk % 2, chunk // 2
-            t = work.tile([P, 4, 1024], BF16, name="xraw", tag="xraw", bufs=XRAW_BUFS)
-            nc.sync.dma_start(out=t[:], in_=xv[tower][:, 4 * j:4 * j + 4, 1024 * gp:1024 * gp + 1024])
-            xraw[rho] = t
+        def load_until(stop):
+            while state["next_load"] < min(stop, 2 * NCHUNK):
+                rho = state["next_load"]
+                i, gp = rho // 2, rho % 2
+                t = work.tile([P, 4, 1024], BF16, name="xraw", tag="xraw", bufs=XRAW_BUFS)
+                nc.sync.dma_start(
+                    out=t[:], in_=xv[i % 2][:, 4 * (i // 2):4 * (i // 2) + 4, 1024 * gp:1024 * gp + 1024])
+                xraw[rho] = t
+                state["next_load"] = rho + 1
 
-        def raw_words(rho):
-            return xraw[rho][:].bitcast(F32).rearrange("p r (g m u) -> p r g m u", g=2, u=2)
+        def raw_words(i, g):
+            w = xraw[2 * i + g // 2][:].bitcast(F32).rearrange("p r (g m u) -> p r g m u", g=2, u=2)
+            return w[:, :, g % 2]
 
-        def sort(rho):
-            words = raw_words(rho)
-            for g2 in range(2):
-                s = work.tile([P, 4, 2, P], F32, name="xs", tag="xs", bufs=4)
-                nc.vector.tensor_copy(out=s[:], in_=words[:, :, g2].rearrange("p r m u -> p r u m"))
-                xs[(rho, g2)] = s
-            xraw.pop(rho)
+        def sort(i, g):
+            s = work.tile([P, 4, 2, P], F32, name="xs", tag="xs", bufs=4)
+            nc.vector.tensor_copy(out=s[:], in_=raw_words(i, g).rearrange("p r m u -> p r u m"))
+            xs[(i, g)] = s
 
-        def trun(rho):
-            for g2 in range(2):
-                grouped = work.tile([P, 512, 4], BF16, name="xg", tag="xg", bufs=4, align_bytes=64)
-                xg[(rho, g2)] = grouped
-                gw = grouped[:].rearrange("p n t -> p (n t)").bitcast(F32).rearrange(
-                    "p (r n u) -> p r n u", r=4, u=2)
-                for rp in range(2):
-                    tp = psum.tile([P, 2, 2, P], F32, name="tp", tag="tp", bufs=4)
-                    for r2 in range(2):
-                        for u in range(2):
-                            if rho < NRAW:
-                                src = raw_words(rho)[:, 2 * rp + r2, g2, :, u]
-                            else:
-                                src = xs[(rho, g2)][:, 2 * rp + r2, u, :]
-                            nc.tensor.transpose(tp[:, r2, u, :], src, ident[:])
-                    nc.scalar.copy(out=gw[:, 2 * rp:2 * rp + 2], in_=tp[:].rearrange("p r u n -> p r n u"))
-                if rho >= NRAW:
-                    xs.pop((rho, g2))
-            if rho < NRAW:
-                xraw.pop(rho)
+        def trun(i, g, first_bank=None):
+            grouped = work.tile([P, 512, 4], BF16, name="xg", tag="xg", bufs=4, align_bytes=64)
+            xg[(i, g)] = grouped
+            gw = grouped[:].rearrange("p n t -> p (n t)").bitcast(F32).rearrange(
+                "p (r n u) -> p r n u", r=4, u=2)
+            for rp in range(2):
+                tp = bank([P, 2, 2, P], None if first_bank is None else first_bank + rp)
+                for r2 in range(2):
+                    for u in range(2):
+                        if i < RAW_CHUNKS:
+                            src = raw_words(i, g)[:, 2 * rp + r2, :, u]
+                        else:
+                            src = xs[(i, g)][:, 2 * rp + r2, u, :]
+                        nc.tensor.transpose(tp[:, r2, u, :], src, ident[:])
+                nc.scalar.copy(out=gw[:, 2 * rp:2 * rp + 2], in_=tp[:].rearrange("p r u n -> p r n u"))
 
-        def qx(rho, g2):
-            chunk, gp = rho // 2, rho % 2
-            g = 2 * gp + g2
+        def qx(i, g):
             if g == 0:
-                xq[chunk] = work.tile([P, 4, 512], U32, name="xq", tag="xq", bufs=2, align_bytes=64)
-                xsc[chunk] = work.tile([P, 4, 512], U8, name="xsc", tag="xsc", bufs=2, align_bytes=64)
+                xq[i] = work.tile([P, 4, 512], U32, name="xq", tag="xq", bufs=2, align_bytes=64)
+                xsc[i] = work.tile([P, 4, 512], U8, name="xsc", tag="xsc", bufs=2, align_bytes=64)
             nc.vector.quantize_mx(
-                out=xq[chunk][:, g, :].bitcast(FP8X4),
-                scales=xsc[chunk][:, g, :],
-                in_=xg.pop((rho, g2))[:].rearrange("p n t -> p (n t)"),
+                out=xq[i][:, g, :].bitcast(FP8X4),
+                scales=xsc[i][:, g, :],
+                in_=xg[(i, g)][:].rearrange("p n t -> p (n t)"),
             )
 
-        def mm1(acc, tau, t, g):
-            chunk, G = tau // 2, tau % 2
-            c = 4 * G + t
+        def mm1(acc, i, c, g):
             nc.tensor.matmul_mx(
                 out=acc[:],
                 lhsT=w1q[:, g, P * c:P * c + P].bitcast(FP8X4),
                 lhsT_scale=w1s[:, g, P * c:P * c + P],
-                rhs=xq[chunk][:, g, :].bitcast(FP8X4),
-                rhs_scale=xsc[chunk][:, g, :],
+                rhs=xq[i][:, g, :].bitcast(FP8X4),
+                rhs_scale=xsc[i][:, g, :],
                 start=(g == 0),
                 stop=(g == 3),
             )
 
-        def hout(acc, tau, t):
-            c = 4 * (tau % 2) + t
-            if t == 0:
-                hT[tau] = work.tile([P, 4, 512], BF16, name="hT", tag="hT", bufs=2)
-            nc.scalar.activation(out=hT[tau][:, t, :], in_=acc[:], func=ACT.Relu, bias=b1f[:, c:c + 1], scale=1.0)
+        def hout(acc, i, c):
+            if c % 4 == 0:
+                hT[(i, c // 4)] = work.tile([P, 4, 512], BF16, name="hT", tag="hT", bufs=2)
+            nc.scalar.activation(out=hT[(i, c // 4)][:, c % 4, :], in_=acc[:], func=ACT.Relu,
+                                 bias=b1f[:, c:c + 1], scale=1.0)
 
-        def s1(tau, t):
-            acc = psum.tile([P, 512], F32, name="ps1", tag="ps1", bufs=3)
+        def s1(i, c):
+            acc = bank([P, 512])
             for g in range(4):
-                mm1(acc, tau, t, g)
-            hout(acc, tau, t)
+                mm1(acc, i, c, g)
+            hout(acc, i, c)
 
-        def head_open(tau):
-            for t in range(3):
-                hacc[(tau, t)] = psum.tile([P, 512], F32, name="ps1", tag="ps1", bufs=3)
-            hacc[(tau, 3)] = psum.tile([P, 512], F32, name="ps2", tag="ps2", bufs=1)
-
-        def head_pass(tau, g):
+        def head_open(G):
             for t in range(4):
-                mm1(hacc[(tau, t)], tau, t, g)
+                hacc[(G, t)] = bank([P, 512], 4 + t)
 
-        def head_close(tau):
+        def head_pass(G, g):
             for t in range(4):
-                hout(hacc.pop((tau, t)), tau, t)
+                mm1(hacc[(G, t)], 0, 4 * G + t, g)
 
-        def hint(tau, lo=0, hi=512):
+        def head_close(G):
+            for t in range(4):
+                hout(hacc[(G, t)], 0, 4 * G + t)
+
+        def hint(i, G, lo=0, hi=512):
             if lo == 0:
-                hg[tau] = work.tile([P, 512, 4], BF16, name="hg", tag="hg", bufs=2, align_bytes=64)
-            nc.vector.tensor_copy(out=hg[tau][:, lo:hi, :], in_=hT[tau][:, :, lo:hi].rearrange("p t n -> p n t"))
+                hg[(i, G)] = work.tile([P, 512, 4], BF16, name="hg", tag="hg", bufs=2, align_bytes=64)
+            nc.vector.tensor_copy(out=hg[(i, G)][:, lo:hi, :],
+                                  in_=hT[(i, G)][:, :, lo:hi].rearrange("p t n -> p n t"))
 
-        def qh(tau, lo=0, hi=512):
-            chunk, G = tau // 2, tau % 2
+        def qh(i, G, lo=0, hi=512):
             if G == 0 and lo == 0:
-                hq[chunk] = work.tile([P, 2, 512], U32, name="hq", tag="hq", bufs=2, align_bytes=64)
-                hsc[chunk] = work.tile([P, 2, 512], U8, name="hsc", tag="hsc", bufs=2, align_bytes=64)
+                hq[i] = work.tile([P, 2, 512], U32, name="hq", tag="hq", bufs=2, align_bytes=64)
+                hsc[i] = work.tile([P, 2, 512], U8, name="hsc", tag="hsc", bufs=2, align_bytes=64)
             nc.vector.quantize_mx(
-                out=hq[chunk][:, G, lo:hi].bitcast(FP8X4),
-                scales=hsc[chunk][:, G, lo:hi],
-                in_=hg[tau][:, lo:hi, :].rearrange("p n t -> p (n t)"),
+                out=hq[i][:, G, lo:hi].bitcast(FP8X4),
+                scales=hsc[i][:, G, lo:hi],
+                in_=hg[(i, G)][:, lo:hi, :].rearrange("p n t -> p (n t)"),
             )
 
-        def s2(sig, spare=False):
-            chunk, rp = sig // 2, sig % 2
-            if spare:
-                acc = psum.tile([P, 2, Z], F32, name="tp", tag="tp", bufs=4)
-            else:
-                acc = psum.tile([P, 2, Z], F32, name="ps2", tag="ps2", bufs=1)
+        def s2(i, rp):
+            acc = bank([P, 2, Z])
             for r2 in range(2):
                 r = 2 * rp + r2
                 for G in range(2):
                     nc.tensor.matmul_mx(
                         out=acc[:, r2, :],
-                        lhsT=hq[chunk][:, G, P * r:P * r + P].bitcast(FP8X4),
-                        lhsT_scale=hsc[chunk][:, G, P * r:P * r + P],
+                        lhsT=hq[i][:, G, P * r:P * r + P].bitcast(FP8X4),
+                        lhsT_scale=hsc[i][:, G, P * r:P * r + P],
                         rhs=w2q[:, Z * G:Z * G + Z].bitcast(FP8X4),
                         rhs_scale=w2s[:, Z * G:Z * G + Z],
                         start=(G == 0),
                         stop=(G == 1),
                     )
-            ps2[sig] = acc
+            ps2[(i, rp)] = acc
 
-        def maxb(sig):
-            mt[sig] = work.tile([P, 2, Z], F32, name="mt", tag="mt", bufs=4)
-            nc.vector.tensor_tensor(out=mt[sig][:], in0=ps2.pop(sig)[:], in1=nb2[:], op=ALU.max)
+        def maxb(i, rp):
+            mt[(i, rp)] = work.tile([P, 2, Z], F32, name="mt", tag="mt", bufs=4)
+            nc.vector.tensor_tensor(out=mt[(i, rp)][:], in0=ps2[(i, rp)][:], in1=nb2[:], op=ALU.max)
 
-        def diff(sig):
-            dt_[sig] = work.tile([P, 2, Z], F32, name="dd", tag="dd", bufs=2)
-            nc.vector.tensor_tensor(out=dt_[sig][:], in0=mt.pop(sig - 2)[:], in1=mt.pop(sig)[:], op=ALU.subtract)
+        def diff(i, rp):
+            dd[(i, rp)] = work.tile([P, 2, Z], F32, name="dd", tag="dd", bufs=2)
+            nc.vector.tensor_tensor(out=dd[(i, rp)][:], in0=mt[(i - 1, rp)][:], in1=mt[(i, rp)][:],
+                                    op=ALU.subtract)
 
-        def sq(sig):
-            chunk, rp = sig // 2, sig % 2
-            j = chunk // 2
-            d = dt_.pop(sig)
+        def sq(i, rp):
             for r2 in range(2):
-                s = 4 * j + 2 * rp + r2
+                s = 4 * (i // 2) + 2 * rp + r2
                 junk = work.tile([P, Z], F32, name="junk", tag="junk", bufs=2)
-                nc.scalar.activation(out=junk[:], in_=d[:, r2, :], func=ACT.Square, scale=1.0 / 16.0,
+                nc.scalar.activation(out=junk[:], in_=dd[(i, rp)][:, r2, :], func=ACT.Square, scale=1.0 / 16.0,
                                      accum_out=res[:, s:s + 1])
 
         def w1_load(G, g):
@@ -228,7 +217,7 @@ def tile_querysiamese_pa_l_kernel(tc, xp1, xp2, W1, b1, W2, b2, q_energy, out):
         def w1_copy(G, g, eng):
             t = work.tile([P, 2048], BF16, name="w1g", tag="w1g", bufs=3, align_bytes=64)
             dst = t[:].rearrange("p (t m j) -> p t m j", t=4, j=4)
-            src = w1raw.pop((G, g))[:].rearrange("p j (m t) -> p t m j", t=4)
+            src = w1raw[(G, g)][:].rearrange("p j (m t) -> p t m j", t=4)
             if eng == 0:
                 nc.vector.tensor_copy(out=dst, in_=src)
             else:
@@ -239,62 +228,71 @@ def tile_querysiamese_pa_l_kernel(tc, xp1, xp2, W1, b1, W2, b2, q_energy, out):
             nc.vector.quantize_mx(
                 out=w1q[:, g, 512 * G:512 * G + 512].bitcast(FP8X4),
                 scales=w1s[:, g, 512 * G:512 * G + 512],
-                in_=w1g.pop((G, g))[:],
+                in_=w1g[(G, g)][:],
             )
 
-        def step(tau):
-            sig = tau - 3
-            live = 0 <= tau < NSTEP
-            second = 0 <= sig < NSTEP and (sig // 2) % 2 == 1
-            if 0 <= sig < NSTEP:
-                maxb(sig)
-            if live:
-                s1(tau, 0)
-                s1(tau, 1)
-            if 0 <= tau - 1 < NSTEP:
-                hint(tau - 1)
-            if second:
-                diff(sig)
-            if 0 <= tau + 2 < NSTEP:
-                trun(tau + 2)
-            if NRAW <= tau + 3 < NSTEP:
-                sort(tau + 3)
-            if 0 <= tau - 1 < NSTEP:
-                qh(tau - 1)
-            if 0 <= tau + 2 < NSTEP:
-                qx(tau + 2, 0)
-            if live:
-                s1(tau, 2)
-            if second:
-                sq(sig)
-            if live:
-                s1(tau, 3)
-            if 0 <= tau + 2 < NSTEP:
-                qx(tau + 2, 1)
-            if 0 <= tau - 2 < NSTEP:
-                s2(tau - 2)
-            while tau >= 0 and state["next_load"] < min(tau + XRAW_BUFS + 3, NSTEP):
-                load(state["next_load"])
-                state["next_load"] = state["next_load"] + 1
+        def period(i):
+            nxt = i + 1 < NCHUNK
+            if i >= 2:
+                maxb(i - 2, 1)
+            s1(i, 0)
+            s1(i, 1)
+            hint(i - 1, 1)
+            if i >= 2 and i % 2 == 1:
+                diff(i - 2, 1)
+            if nxt:
+                sort(i + 1, 0)
+                sort(i + 1, 1)
+            qh(i - 1, 1)
+            s1(i, 2)
+            if i >= 2 and i % 2 == 1:
+                sq(i - 2, 1)
+            s1(i, 3)
+            if nxt:
+                sort(i + 1, 2)
+                sort(i + 1, 3)
+                load_until(2 * i + 4 + XRAW_BUFS)
+            s2(i - 1, 0)
+            maxb(i - 1, 0)
+            if nxt:
+                for g in range(4):
+                    trun(i + 1, g)
+            hint(i, 0)
+            if i % 2 == 0:
+                diff(i - 1, 0)
+            if nxt:
+                qx(i + 1, 0)
+            qh(i, 0)
+            if nxt:
+                qx(i + 1, 1)
+                qx(i + 1, 2)
+                qx(i + 1, 3)
+            s1(i, 4)
+            s1(i, 5)
+            if i % 2 == 0:
+                sq(i - 1, 0)
+            s1(i, 6)
+            s1(i, 7)
+            s2(i - 1, 1)
 
-        load(0)
+        load_until(1)
         w1_load(0, 0)
         w1_load(0, 1)
-        load(1)
+        load_until(2)
         w1_load(0, 2)
         w1_load(0, 3)
         for g in range(4):
             w1_load(1, g)
-        for rho in range(2, XRAW_BUFS):
-            load(rho)
+        load_until(XRAW_BUFS)
 
-        psb = psum.tile([P, 2, Z], F32, name="ps2", tag="ps2", bufs=1)
+        psb = bank([P, 2, Z], 4)
         for r2 in range(2):
             nc.tensor.matmul(out=psb[:, r2, :], lhsT=negones[:], rhs=brow[:], start=True, stop=True)
         nc.vector.tensor_copy(out=nb2[:], in_=psb[:])
         nc.vector.tensor_copy(out=b1f[:], in_=b1t[:].rearrange("p g t -> p (g t)"))
 
-        trun(0)
+        trun(0, 0, 0)
+        trun(0, 1, 2)
         w1_copy(0, 0, 0)
         qx(0, 0)
         w1_quant(0, 0)
@@ -302,15 +300,16 @@ def tile_querysiamese_pa_l_kernel(tc, xp1, xp2, W1, b1, W2, b2, q_energy, out):
         w1_copy(0, 1, 1)
         head_open(0)
         head_pass(0, 0)
-        trun(1)
+        trun(0, 2, 0)
+        trun(0, 3, 2)
         w1_quant(0, 1)
         head_pass(0, 1)
         w1_copy(0, 2, 0)
-        qx(1, 0)
+        qx(0, 2)
         w1_quant(0, 2)
         head_pass(0, 2)
         w1_copy(0, 3, 1)
-        qx(1, 1)
+        qx(0, 3)
         w1_copy(1, 0, 0)
         w1_quant(0, 3)
         head_pass(0, 3)
@@ -328,41 +327,43 @@ def tile_querysiamese_pa_l_kernel(tc, xp1, xp2, W1, b1, W2, b2, q_energy, out):
         head_pass(1, 1)
         w1_copy(1, 3, 0)
         w1_quant(1, 2)
-        trun(2)
+        trun(1, 0, 0)
+        trun(1, 1, 2)
         head_pass(1, 2)
         w1_quant(1, 3)
-        qx(2, 0)
-        qx(2, 1)
-        trun(3)
+        qx(1, 0)
+        qx(1, 1)
+        trun(1, 2, 0)
+        trun(1, 3, 2)
+        load_until(4 + XRAW_BUFS)
         head_pass(1, 3)
         head_close(1)
-        sort(4)
-        qx(3, 0)
-        qx(3, 1)
-        hint(0)
+        qx(1, 2)
+        qx(1, 3)
+        hint(0, 0)
         w2g = work.tile([P, 2, Z, 4], BF16, name="w1g", tag="w1g", bufs=3, align_bytes=64)
         nc.vector.tensor_copy(out=w2g[:], in_=w2raw[:].rearrange("p g j z -> p g z j"))
-        qh(0)
+        qh(0, 0)
         nc.vector.quantize_mx(out=w2q[:].bitcast(FP8X4), scales=w2s[:],
                               in_=w2g[:].rearrange("p g z j -> p (g z j)"))
 
-        for tau in range(2, NSTEP):
-            step(tau)
+        for i in range(1, NCHUNK):
+            period(i)
 
-        last = NSTEP - 1
-        maxb(last - 2)
-        hint(last, 0, 256)
-        hint(last, 256, 512)
-        qh(last, 0, 256)
-        qh(last, 256, 512)
-        s2(last - 1)
-        s2(last, True)
-        maxb(last - 1)
-        maxb(last)
-        diff(last - 1)
-        diff(last)
-        sq(last - 1)
-        sq(last)
+        last = NCHUNK - 1
+        maxb(last - 1, 1)
+        hint(last, 1, 0, 256)
+        hint(last, 1, 256, 512)
+        qh(last, 1, 0, 256)
+        qh(last, 1, 256, 512)
+        s2(last, 0)
+        s2(last, 1)
+        maxb(last, 0)
+        maxb(last, 1)
+        diff(last, 0)
+        diff(last, 1)
+        sq(last, 0)
+        sq(last, 1)
 
         o = keep.tile([P, SUB], F32, name="o", tag="o")
         nc.vector.tensor_tensor(out=o[:], in0=res[:], in1=qt[:], op=ALU.mult)

@@ -19,7 +19,7 @@ NCHUNK = 24
 FLOPS = 2 * 2 * ROWS * (E * F + F * Z)
 
 RAW_CHUNKS = 2
-XRAW_BUFS = 6
+X_BUFS = 3
 
 
 def tile_querysiamese_pa_l_kernel(tc, xp1, xp2, W1, b1, W2, b2, q_energy, out):
@@ -30,7 +30,7 @@ def tile_querysiamese_pa_l_kernel(tc, xp1, xp2, W1, b1, W2, b2, q_energy, out):
         work = ctx.enter_context(tc.tile_pool(name="work", bufs=1))
         psum = ctx.enter_context(tc.psum_pool(name="psum", bufs=1))
 
-        xv = [xp.rearrange("a (b s) k -> (a b) s k", s=SUB) for xp in (xp1, xp2)]
+        xf = [xp.rearrange("a b k -> (a b) k") for xp in (xp1, xp2)]
         state = {"next_load": 0, "bank": 0}
 
         def bank(shape, idx=None):
@@ -60,10 +60,16 @@ def tile_querysiamese_pa_l_kernel(tc, xp1, xp2, W1, b1, W2, b2, q_energy, out):
         w2s = keep.tile([P, 2 * Z], U8, name="w2s", tag="w2s", align_bytes=64)
         nb2 = keep.tile([P, 2, Z], F32, name="nb2", tag="nb2")
         b1f = keep.tile([P, 8], F32, name="b1f", tag="b1f")
-        res = keep.tile([P, SUB], F32, name="res", tag="res")
-        qt = keep.tile([P, SUB], BF16, name="qt", tag="qt")
+        res = keep.tile([P, P], F32, name="res", tag="res")
+        nc.vector.memset(res[:], 0.0)
+        qt = keep.tile([P, P], BF16, name="qt", tag="qt")
+        nc.vector.memset(qt[:], 0.0)
 
-        xraw = {}
+        xa = {}
+        xb = {}
+        xc = {}
+        vs = {}
+        vtr = {}
         xs = {}
         xg = {}
         xq = {}
@@ -79,22 +85,49 @@ def tile_querysiamese_pa_l_kernel(tc, xp1, xp2, W1, b1, W2, b2, q_energy, out):
         w1g = {}
         hacc = {}
 
-        def load_until(stop):
-            while state["next_load"] < min(stop, 2 * NCHUNK):
-                rho = state["next_load"]
-                i, gp = rho // 2, rho % 2
-                t = work.tile([P, 4, 1024], BF16, name="xraw", tag="xraw", bufs=XRAW_BUFS)
-                nc.sync.dma_start(
-                    out=t[:], in_=xv[i % 2][:, 4 * (i // 2):4 * (i // 2) + 4, 1024 * gp:1024 * gp + 1024])
-                xraw[rho] = t
-                state["next_load"] = rho + 1
+        def rows(i):
+            return xf[i % 2][512 * (i // 2):512 * (i // 2) + 512, :]
+
+        def load_a(i):
+            if i < NCHUNK:
+                xa[i] = work.tile([P, 4, 1024], BF16, name="xa", tag="xa", bufs=X_BUFS)
+                nc.sync.dma_start(out=xa[i][:], in_=rows(i)[:, 0:1024].rearrange("(r p) k -> p r k", p=P))
+
+        def load_b(i):
+            if i < NCHUNK:
+                width = 1024 if i < RAW_CHUNKS else 512
+                xb[i] = work.tile([P, 4, width], BF16, name="xb", tag="xb", bufs=X_BUFS)
+                nc.sync.dma_start(out=xb[i][:], in_=rows(i)[:, 1024:1024 + width].rearrange("(r p) k -> p r k", p=P))
+
+        def load_c(i):
+            if RAW_CHUNKS <= i < NCHUNK:
+                xc[i] = work.tile([P, 16, P], BF16, name="xc", tag="xc", bufs=X_BUFS)
+                for Q in range(4):
+                    nc.sync.dma_start(
+                        out=xc[i][32 * Q:32 * Q + 32, :, :],
+                        in_=rows(i)[:, 1536 + P * Q:1536 + P * Q + P].rearrange("(n j) k -> j n k", j=32))
 
         def raw_words(i, g):
-            w = xraw[2 * i + g // 2][:].bitcast(F32).rearrange("p r (g m u) -> p r g m u", g=2, u=2)
+            src = xa[i] if g < 2 else xb[i]
+            w = src[:].bitcast(F32).rearrange("p r (g m u) -> p r g m u", m=P, u=2)
             return w[:, :, g % 2]
 
+        def vsort(i):
+            vs[i] = work.tile([P, 16, 2, 32], F32, name="vs", tag="vs", bufs=1, align_bytes=64)
+            nc.scalar.copy(out=vs[i][:], in_=xc[i][:].bitcast(F32).rearrange("p n (i u) -> p n u i", u=2))
+
+        def vt(i):
+            vtr[i] = work.tile([P, 1024], F32, name="vtr", tag="vtr", bufs=1, align_bytes=64)
+            nc.vector.transpose(out=vtr[i][:], in_=vs[i][:].rearrange("p n u i -> p (n u i)"))
+
+        def vint(i):
+            grouped = work.tile([P, 512, 4], BF16, name="xg", tag="xg", bufs=4, align_bytes=64)
+            xg[(i, 3)] = grouped
+            gw = grouped[:].rearrange("p n t -> p (n t)").bitcast(F32).rearrange("p (n j u) -> p n j u", n=16, u=2)
+            nc.scalar.copy(out=gw, in_=vtr[i][:].rearrange("p (n u j) -> p n j u", n=16, u=2))
+
         def sort(i, g):
-            s = work.tile([P, 4, 2, P], F32, name="xs", tag="xs", bufs=4)
+            s = work.tile([P, 4, 2, P], F32, name="xs", tag="xs", bufs=3)
             nc.vector.tensor_copy(out=s[:], in_=raw_words(i, g).rearrange("p r m u -> p r u m"))
             xs[(i, g)] = s
 
@@ -237,26 +270,31 @@ def tile_querysiamese_pa_l_kernel(tc, xp1, xp2, W1, b1, W2, b2, q_energy, out):
                 maxb(i - 2, 1)
             s1(i, 0)
             s1(i, 1)
+            if nxt:
+                vsort(i + 1)
+                load_c(i + 1 + X_BUFS)
             hint(i - 1, 1)
             if i >= 2 and i % 2 == 1:
                 diff(i - 2, 1)
             if nxt:
                 sort(i + 1, 0)
                 sort(i + 1, 1)
+                load_a(i + 1 + X_BUFS)
             qh(i - 1, 1)
+            if nxt:
+                sort(i + 1, 2)
+                load_b(i + 1 + X_BUFS)
+                vt(i + 1)
             s1(i, 2)
             if i >= 2 and i % 2 == 1:
                 sq(i - 2, 1)
             s1(i, 3)
-            if nxt:
-                sort(i + 1, 2)
-                sort(i + 1, 3)
-                load_until(2 * i + 4 + XRAW_BUFS)
             s2(i - 1, 0)
             maxb(i - 1, 0)
             if nxt:
-                for g in range(4):
+                for g in range(3):
                     trun(i + 1, g)
+                vint(i + 1)
             hint(i, 0)
             if i % 2 == 0:
                 diff(i - 1, 0)
@@ -275,15 +313,18 @@ def tile_querysiamese_pa_l_kernel(tc, xp1, xp2, W1, b1, W2, b2, q_energy, out):
             s1(i, 7)
             s2(i - 1, 1)
 
-        load_until(1)
+        load_a(0)
         w1_load(0, 0)
         w1_load(0, 1)
-        load_until(2)
+        load_b(0)
         w1_load(0, 2)
         w1_load(0, 3)
         for g in range(4):
             w1_load(1, g)
-        load_until(XRAW_BUFS)
+        for i in range(1, X_BUFS):
+            load_a(i)
+            load_b(i)
+            load_c(i)
 
         psb = bank([P, 2, Z], 4)
         for r2 in range(2):
@@ -317,7 +358,10 @@ def tile_querysiamese_pa_l_kernel(tc, xp1, xp2, W1, b1, W2, b2, q_energy, out):
         head_close(0)
         w2raw = work.tile([P, 2, 4, Z], BF16, name="w1raw", tag="w1raw", bufs=8)
         nc.sync.dma_start(out=w2raw[:], in_=W2.rearrange("(g p j) z -> p g j z", g=2, j=4))
-        nc.sync.dma_start(out=qt[:], in_=q_energy.rearrange("a (b s) -> (a b) s", s=SUB))
+        nc.sync.dma_start(out=qt[0:SUB, :], in_=q_energy.rearrange("a (b p) -> (a b) p", p=P))
+        load_a(X_BUFS)
+        load_b(X_BUFS)
+        load_c(X_BUFS)
 
         w1_copy(1, 2, 0)
         w1_quant(1, 0)
@@ -335,7 +379,9 @@ def tile_querysiamese_pa_l_kernel(tc, xp1, xp2, W1, b1, W2, b2, q_energy, out):
         qx(1, 1)
         trun(1, 2, 0)
         trun(1, 3, 2)
-        load_until(4 + XRAW_BUFS)
+        load_a(1 + X_BUFS)
+        load_b(1 + X_BUFS)
+        load_c(1 + X_BUFS)
         head_pass(1, 3)
         head_close(1)
         qx(1, 2)
@@ -365,6 +411,10 @@ def tile_querysiamese_pa_l_kernel(tc, xp1, xp2, W1, b1, W2, b2, q_energy, out):
         sq(last, 0)
         sq(last, 1)
 
-        o = keep.tile([P, SUB], F32, name="o", tag="o")
-        nc.vector.tensor_tensor(out=o[:], in0=res[:], in1=qt[:], op=ALU.mult)
-        nc.sync.dma_start(out=out.rearrange("a (b s) -> (a b) s", s=SUB), in_=o[:])
+        rT = bank([P, P])
+        nc.tensor.transpose(rT[:], res[:], ident[:])
+        o = keep.tile([P, P], F32, name="o", tag="o")
+        nc.vector.tensor_tensor(out=o[:], in0=rT[:], in1=qt[:], op=ALU.mult)
+        outv = out.rearrange("a (b p) -> (a b) p", p=P)
+        nc.sync.dma_start(out=outv[0:32, :], in_=o[0:32, :])
+        nc.sync.dma_start(out=outv[32:SUB, :], in_=o[32:SUB, :])

@@ -20,6 +20,12 @@ FLOPS = 2 * 2 * ROWS * (E * F + F * Z)
 
 RAW_CHUNKS = 2
 X_BUFS = 3
+VPASS = ((2, 3), (2, 3))
+VSORT_ON_VECTOR = (3,)
+XB_BUFS = 2
+XC_BUFS = 6
+XS_BUFS = 2
+V_BUFS = 2
 
 
 def tile_querysiamese_pa_l_kernel(tc, xp1, xp2, W1, b1, W2, b2, q_energy, out):
@@ -85,6 +91,12 @@ def tile_querysiamese_pa_l_kernel(tc, xp1, xp2, W1, b1, W2, b2, q_energy, out):
         w1g = {}
         hacc = {}
 
+        def vpasses(i):
+            return () if i < RAW_CHUNKS else VPASS[i % 2]
+
+        def tpasses(i):
+            return [g for g in range(4) if g not in vpasses(i)]
+
         def rows(i):
             return xf[i % 2][512 * (i // 2):512 * (i // 2) + 512, :]
 
@@ -94,40 +106,45 @@ def tile_querysiamese_pa_l_kernel(tc, xp1, xp2, W1, b1, W2, b2, q_energy, out):
                 nc.sync.dma_start(out=xa[i][:], in_=rows(i)[:, 0:1024].rearrange("(r p) k -> p r k", p=P))
 
         def load_b(i):
-            if i < NCHUNK:
+            if i < NCHUNK and 2 in tpasses(i):
                 width = 1024 if i < RAW_CHUNKS else 512
-                xb[i] = work.tile([P, 4, width], BF16, name="xb", tag="xb", bufs=X_BUFS)
+                xb[i] = work.tile([P, 4, width], BF16, name="xb", tag="xb", bufs=XB_BUFS)
                 nc.sync.dma_start(out=xb[i][:], in_=rows(i)[:, 1024:1024 + width].rearrange("(r p) k -> p r k", p=P))
 
         def load_c(i):
-            if RAW_CHUNKS <= i < NCHUNK:
-                xc[i] = work.tile([P, 16, P], BF16, name="xc", tag="xc", bufs=X_BUFS)
-                for Q in range(4):
-                    nc.sync.dma_start(
-                        out=xc[i][32 * Q:32 * Q + 32, :, :],
-                        in_=rows(i)[:, 1536 + P * Q:1536 + P * Q + P].rearrange("(n j) k -> j n k", j=32))
+            if i < NCHUNK:
+                for g in vpasses(i):
+                    xc[(i, g)] = work.tile([P, 16, P], BF16, name="xc", tag="xc", bufs=XC_BUFS)
+                    for Q in range(4):
+                        nc.sync.dma_start(
+                            out=xc[(i, g)][32 * Q:32 * Q + 32, :, :],
+                            in_=rows(i)[:, 512 * g + P * Q:512 * g + P * Q + P].rearrange("(n j) k -> j n k", j=32))
 
         def raw_words(i, g):
             src = xa[i] if g < 2 else xb[i]
             w = src[:].bitcast(F32).rearrange("p r (g m u) -> p r g m u", m=P, u=2)
             return w[:, :, g % 2]
 
-        def vsort(i):
-            vs[i] = work.tile([P, 16, 2, 32], F32, name="vs", tag="vs", bufs=1, align_bytes=64)
-            nc.scalar.copy(out=vs[i][:], in_=xc[i][:].bitcast(F32).rearrange("p n (i u) -> p n u i", u=2))
+        def vsort(i, g):
+            vs[(i, g)] = work.tile([P, 16, 2, 32], F32, name="vs", tag="vs", bufs=V_BUFS, align_bytes=64)
+            src = xc[(i, g)][:].bitcast(F32).rearrange("p n (i u) -> p n u i", u=2)
+            if g in VSORT_ON_VECTOR:
+                nc.vector.tensor_copy(out=vs[(i, g)][:], in_=src)
+            else:
+                nc.scalar.copy(out=vs[(i, g)][:], in_=src)
 
-        def vt(i):
-            vtr[i] = work.tile([P, 1024], F32, name="vtr", tag="vtr", bufs=1, align_bytes=64)
-            nc.vector.transpose(out=vtr[i][:], in_=vs[i][:].rearrange("p n u i -> p (n u i)"))
+        def vt(i, g):
+            vtr[(i, g)] = work.tile([P, 1024], F32, name="vtr", tag="vtr", bufs=V_BUFS, align_bytes=64)
+            nc.vector.transpose(out=vtr[(i, g)][:], in_=vs[(i, g)][:].rearrange("p n u i -> p (n u i)"))
 
-        def vint(i):
+        def vint(i, g):
             grouped = work.tile([P, 512, 4], BF16, name="xg", tag="xg", bufs=4, align_bytes=64)
-            xg[(i, 3)] = grouped
+            xg[(i, g)] = grouped
             gw = grouped[:].rearrange("p n t -> p (n t)").bitcast(F32).rearrange("p (n j u) -> p n j u", n=16, u=2)
-            nc.scalar.copy(out=gw, in_=vtr[i][:].rearrange("p (n u j) -> p n j u", n=16, u=2))
+            nc.scalar.copy(out=gw, in_=vtr[(i, g)][:].rearrange("p (n u j) -> p n j u", n=16, u=2))
 
         def sort(i, g):
-            s = work.tile([P, 4, 2, P], F32, name="xs", tag="xs", bufs=3)
+            s = work.tile([P, 4, 2, P], F32, name="xs", tag="xs", bufs=XS_BUFS)
             nc.vector.tensor_copy(out=s[:], in_=raw_words(i, g).rearrange("p r m u -> p r u m"))
             xs[(i, g)] = s
 
@@ -265,48 +282,56 @@ def tile_querysiamese_pa_l_kernel(tc, xp1, xp2, W1, b1, W2, b2, q_energy, out):
             )
 
         def period(i):
-            nxt = i + 1 < NCHUNK
+            n = i + 1
+            tg = tpasses(n) if n < NCHUNK else []
+            vg = [g for g in vpasses(n)] if n < NCHUNK else []
             if i >= 2:
                 maxb(i - 2, 1)
             s1(i, 0)
             s1(i, 1)
-            if nxt:
-                vsort(i + 1)
-                load_c(i + 1 + X_BUFS)
+            for g in vg:
+                if g not in VSORT_ON_VECTOR:
+                    vsort(n, g)
             hint(i - 1, 1)
             if i >= 2 and i % 2 == 1:
                 diff(i - 2, 1)
-            if nxt:
-                sort(i + 1, 0)
-                sort(i + 1, 1)
-                load_a(i + 1 + X_BUFS)
+            for g in tg[0:2]:
+                sort(n, g)
+            load_a(n + X_BUFS)
             qh(i - 1, 1)
-            if nxt:
-                sort(i + 1, 2)
-                load_b(i + 1 + X_BUFS)
-                vt(i + 1)
+            for g in tg[2:]:
+                sort(n, g)
+            load_b(n + X_BUFS)
+            for g in vg:
+                if g in VSORT_ON_VECTOR:
+                    vsort(n, g)
+            load_c(n + X_BUFS)
+            for g in vg:
+                vt(n, g)
             s1(i, 2)
             if i >= 2 and i % 2 == 1:
                 sq(i - 2, 1)
             s1(i, 3)
             s2(i - 1, 0)
             maxb(i - 1, 0)
-            if nxt:
-                for g in range(3):
-                    trun(i + 1, g)
-                vint(i + 1)
+            for g in tg:
+                trun(n, g)
             hint(i, 0)
             if i % 2 == 0:
                 diff(i - 1, 0)
-            if nxt:
-                qx(i + 1, 0)
+            for g in tg[0:1]:
+                qx(n, g)
             qh(i, 0)
-            if nxt:
-                qx(i + 1, 1)
-                qx(i + 1, 2)
-                qx(i + 1, 3)
+            for g in tg[1:]:
+                qx(n, g)
             s1(i, 4)
+            for g in vg[0:1]:
+                vint(n, g)
+                qx(n, g)
             s1(i, 5)
+            for g in vg[1:]:
+                vint(n, g)
+                qx(n, g)
             if i % 2 == 0:
                 sq(i - 1, 0)
             s1(i, 6)

from contextlib import ExitStack

import concourse.mybir as mybir
from concourse.masks import make_identity

F32 = mybir.dt.float32
BF16 = mybir.dt.bfloat16
U32 = mybir.dt.uint32
U8 = mybir.dt.uint8
FP8X4 = mybir.dt.float8_e4m3fn_x4
ACT = mybir.ActivationFunctionType
ALU = mybir.AluOpType

P = 128
E, F, Z = 2048, 1024, 256
ROWS = 6144
SUB = ROWS // P
NCHUNK = 24
FLOPS = 2 * 2 * ROWS * (E * F + F * Z)

RAW_CHUNKS = 2
X_BUFS = 3
VPASS = ((2, 3), (2, 3))
VSORT_ON_VECTOR = (3,)
XB_BUFS = 2
XC_BUFS = 6
XS_BUFS = 2
V_BUFS = 2


def tile_querysiamese_pa_l_kernel(tc, xp1, xp2, W1, b1, W2, b2, q_energy, out):
    nc = tc.nc
    with ExitStack() as ctx:
        ctx.enter_context(tc.manual_schedule())
        keep = ctx.enter_context(tc.tile_pool(name="keep", bufs=1))
        work = ctx.enter_context(tc.tile_pool(name="work", bufs=1))
        psum = ctx.enter_context(tc.psum_pool(name="psum", bufs=1))

        xf = [xp.rearrange("a b k -> (a b) k") for xp in (xp1, xp2)]
        state = {"next_load": 0, "bank": 0}

        def bank(shape, idx=None):
            if idx is None:
                idx = state["bank"] % 8
                state["bank"] = state["bank"] + 1
            return psum.tile(shape, F32, name="bank%d" % idx, tag="bank%d" % idx)

        ident = keep.tile([P, P], F32, name="ident", tag="ident")
        make_identity(nc, ident[:])
        negones = keep.tile([P, P], BF16, name="negones", tag="negones")
        nc.vector.memset(negones[:], -1.0)
        brow = keep.tile([P, Z], BF16, name="brow", tag="brow")
        nc.vector.memset(brow[:], 0.0)
        warm = keep.tile([P, 1], F32, name="warm", tag="warm")
        nc.vector.memset(warm[:], 0.0)
        warm2 = keep.tile([P, 1], F32, name="warm2", tag="warm2")
        nc.scalar.activation(out=warm2[:], in_=warm[:], func=ACT.Relu)

        nc.sync.dma_start(out=brow[0:1, :], in_=b2.rearrange("(o z) -> o z", o=1))
        b1t = keep.tile([P, 2, 4], BF16, name="b1t", tag="b1t")
        nc.sync.dma_start(out=b1t[:], in_=b1.rearrange("(g p t) -> p g t", g=2, t=4))

        w1q = keep.tile([P, 4, F], U32, name="w1q", tag="w1q", align_bytes=64)
        w1s = keep.tile([P, 4, F], U8, name="w1s", tag="w1s", align_bytes=64)
        w2q = keep.tile([P, 2 * Z], U32, name="w2q", tag="w2q", align_bytes=64)
        w2s = keep.tile([P, 2 * Z], U8, name="w2s", tag="w2s", align_bytes=64)
        nb2 = keep.tile([P, 2, Z], F32, name="nb2", tag="nb2")
        b1f = keep.tile([P, 8], F32, name="b1f", tag="b1f")
        res = keep.tile([P, P], F32, name="res", tag="res")
        nc.vector.memset(res[:], 0.0)
        qt = keep.tile([P, P], BF16, name="qt", tag="qt")
        nc.vector.memset(qt[:], 0.0)

        xa = {}
        xb = {}
        xc = {}
        vs = {}
        vtr = {}
        xs = {}
        xg = {}
        xq = {}
        xsc = {}
        hT = {}
        hg = {}
        hq = {}
        hsc = {}
        ps2 = {}
        mt = {}
        dd = {}
        w1raw = {}
        w1g = {}
        hacc = {}

        def vpasses(i):
            return () if i < RAW_CHUNKS else VPASS[i % 2]

        def tpasses(i):
            return [g for g in range(4) if g not in vpasses(i)]

        def rows(i):
            return xf[i % 2][512 * (i // 2):512 * (i // 2) + 512, :]

        def load_a(i):
            if i < NCHUNK:
                xa[i] = work.tile([P, 4, 1024], BF16, name="xa", tag="xa", bufs=X_BUFS)
                nc.sync.dma_start(out=xa[i][:], in_=rows(i)[:, 0:1024].rearrange("(r p) k -> p r k", p=P))

        def load_b(i):
            if i < NCHUNK and 2 in tpasses(i):
                width = 1024 if i < RAW_CHUNKS else 512
                xb[i] = work.tile([P, 4, width], BF16, name="xb", tag="xb", bufs=XB_BUFS)
                nc.sync.dma_start(out=xb[i][:], in_=rows(i)[:, 1024:1024 + width].rearrange("(r p) k -> p r k", p=P))

        def load_c(i):
            if i < NCHUNK:
                for g in vpasses(i):
                    xc[(i, g)] = work.tile([P, 16, P], BF16, name="xc", tag="xc", bufs=XC_BUFS)
                    for Q in range(4):
                        nc.sync.dma_start(
                            out=xc[(i, g)][32 * Q:32 * Q + 32, :, :],
                            in_=rows(i)[:, 512 * g + P * Q:512 * g + P * Q + P].rearrange("(n j) k -> j n k", j=32))

        def raw_words(i, g):
            src = xa[i] if g < 2 else xb[i]
            w = src[:].bitcast(F32).rearrange("p r (g m u) -> p r g m u", m=P, u=2)
            return w[:, :, g % 2]

        def vsort(i, g):
            vs[(i, g)] = work.tile([P, 16, 2, 32], F32, name="vs", tag="vs", bufs=V_BUFS, align_bytes=64)
            src = xc[(i, g)][:].bitcast(F32).rearrange("p n (i u) -> p n u i", u=2)
            if g in VSORT_ON_VECTOR:
                nc.vector.tensor_copy(out=vs[(i, g)][:], in_=src)
            else:
                nc.scalar.copy(out=vs[(i, g)][:], in_=src)

        def vt(i, g):
            vtr[(i, g)] = work.tile([P, 1024], F32, name="vtr", tag="vtr", bufs=V_BUFS, align_bytes=64)
            nc.vector.transpose(out=vtr[(i, g)][:], in_=vs[(i, g)][:].rearrange("p n u i -> p (n u i)"))

        def vint(i, g):
            grouped = work.tile([P, 512, 4], BF16, name="xg", tag="xg", bufs=4, align_bytes=64)
            xg[(i, g)] = grouped
            gw = grouped[:].rearrange("p n t -> p (n t)").bitcast(F32).rearrange("p (n j u) -> p n j u", n=16, u=2)
            nc.scalar.copy(out=gw, in_=vtr[(i, g)][:].rearrange("p (n u j) -> p n j u", n=16, u=2))

        def sort(i, g):
            s = work.tile([P, 4, 2, P], F32, name="xs", tag="xs", bufs=XS_BUFS)
            nc.vector.tensor_copy(out=s[:], in_=raw_words(i, g).rearrange("p r m u -> p r u m"))
            xs[(i, g)] = s

        def trun(i, g, first_bank=None):
            grouped = work.tile([P, 512, 4], BF16, name="xg", tag="xg", bufs=4, align_bytes=64)
            xg[(i, g)] = grouped
            gw = grouped[:].rearrange("p n t -> p (n t)").bitcast(F32).rearrange(
                "p (r n u) -> p r n u", r=4, u=2)
            for rp in range(2):
                tp = bank([P, 2, 2, P], None if first_bank is None else first_bank + rp)
                for r2 in range(2):
                    for u in range(2):
                        if i < RAW_CHUNKS:
                            src = raw_words(i, g)[:, 2 * rp + r2, :, u]
                        else:
                            src = xs[(i, g)][:, 2 * rp + r2, u, :]
                        nc.tensor.transpose(tp[:, r2, u, :], src, ident[:])
                nc.scalar.copy(out=gw[:, 2 * rp:2 * rp + 2], in_=tp[:].rearrange("p r u n -> p r n u"))

        def qx(i, g):
            if g == 0:
                xq[i] = work.tile([P, 4, 512], U32, name="xq", tag="xq", bufs=2, align_bytes=64)
                xsc[i] = work.tile([P, 4, 512], U8, name="xsc", tag="xsc", bufs=2, align_bytes=64)
            nc.vector.quantize_mx(
                out=xq[i][:, g, :].bitcast(FP8X4),
                scales=xsc[i][:, g, :],
                in_=xg[(i, g)][:].rearrange("p n t -> p (n t)"),
            )

        def mm1(acc, i, c, g):
            nc.tensor.matmul_mx(
                out=acc[:],
                lhsT=w1q[:, g, P * c:P * c + P].bitcast(FP8X4),
                lhsT_scale=w1s[:, g, P * c:P * c + P],
                rhs=xq[i][:, g, :].bitcast(FP8X4),
                rhs_scale=xsc[i][:, g, :],
                start=(g == 0),
                stop=(g == 3),
            )

        def hout(acc, i, c):
            if c % 4 == 0:
                hT[(i, c // 4)] = work.tile([P, 4, 512], BF16, name="hT", tag="hT", bufs=2)
            nc.scalar.activation(out=hT[(i, c // 4)][:, c % 4, :], in_=acc[:], func=ACT.Relu,
                                 bias=b1f[:, c:c + 1], scale=1.0)

        def s1(i, c):
            acc = bank([P, 512])
            for g in range(4):
                mm1(acc, i, c, g)
            hout(acc, i, c)

        def head_open(G):
            for t in range(4):
                hacc[(G, t)] = bank([P, 512], 4 + t)

        def head_pass(G, g):
            for t in range(4):
                mm1(hacc[(G, t)], 0, 4 * G + t, g)

        def head_close(G):
            for t in range(4):
                hout(hacc[(G, t)], 0, 4 * G + t)

        def hint(i, G, lo=0, hi=512):
            if lo == 0:
                hg[(i, G)] = work.tile([P, 512, 4], BF16, name="hg", tag="hg", bufs=2, align_bytes=64)
            nc.vector.tensor_copy(out=hg[(i, G)][:, lo:hi, :],
                                  in_=hT[(i, G)][:, :, lo:hi].rearrange("p t n -> p n t"))

        def qh(i, G, lo=0, hi=512):
            if G == 0 and lo == 0:
                hq[i] = work.tile([P, 2, 512], U32, name="hq", tag="hq", bufs=2, align_bytes=64)
                hsc[i] = work.tile([P, 2, 512], U8, name="hsc", tag="hsc", bufs=2, align_bytes=64)
            nc.vector.quantize_mx(
                out=hq[i][:, G, lo:hi].bitcast(FP8X4),
                scales=hsc[i][:, G, lo:hi],
                in_=hg[(i, G)][:, lo:hi, :].rearrange("p n t -> p (n t)"),
            )

        def s2(i, rp):
            acc = bank([P, 2, Z])
            for r2 in range(2):
                r = 2 * rp + r2
                for G in range(2):
                    nc.tensor.matmul_mx(
                        out=acc[:, r2, :],
                        lhsT=hq[i][:, G, P * r:P * r + P].bitcast(FP8X4),
                        lhsT_scale=hsc[i][:, G, P * r:P * r + P],
                        rhs=w2q[:, Z * G:Z * G + Z].bitcast(FP8X4),
                        rhs_scale=w2s[:, Z * G:Z * G + Z],
                        start=(G == 0),
                        stop=(G == 1),
                    )
            ps2[(i, rp)] = acc

        def maxb(i, rp):
            mt[(i, rp)] = work.tile([P, 2, Z], F32, name="mt", tag="mt", bufs=4)
            nc.vector.tensor_tensor(out=mt[(i, rp)][:], in0=ps2[(i, rp)][:], in1=nb2[:], op=ALU.max)

        def diff(i, rp):
            dd[(i, rp)] = work.tile([P, 2, Z], F32, name="dd", tag="dd", bufs=2)
            nc.vector.tensor_tensor(out=dd[(i, rp)][:], in0=mt[(i - 1, rp)][:], in1=mt[(i, rp)][:],
                                    op=ALU.subtract)

        def sq(i, rp):
            for r2 in range(2):
                s = 4 * (i // 2) + 2 * rp + r2
                junk = work.tile([P, Z], F32, name="junk", tag="junk", bufs=2)
                nc.scalar.activation(out=junk[:], in_=dd[(i, rp)][:, r2, :], func=ACT.Square, scale=1.0 / 16.0,
                                     accum_out=res[:, s:s + 1])

        def w1_load(G, g):
            t = work.tile([P, 4, 512], BF16, name="w1raw", tag="w1raw", bufs=8)
            nc.sync.dma_start(
                out=t[:],
                in_=W1[512 * g:512 * g + 512, 512 * G:512 * G + 512].rearrange("(p j) c -> p j c", j=4))
            w1raw[(G, g)] = t

        def w1_copy(G, g, eng):
            t = work.tile([P, 2048], BF16, name="w1g", tag="w1g", bufs=3, align_bytes=64)
            dst = t[:].rearrange("p (t m j) -> p t m j", t=4, j=4)
            src = w1raw[(G, g)][:].rearrange("p j (m t) -> p t m j", t=4)
            if eng == 0:
                nc.vector.tensor_copy(out=dst, in_=src)
            else:
                nc.scalar.copy(out=dst, in_=src)
            w1g[(G, g)] = t

        def w1_quant(G, g):
            nc.vector.quantize_mx(
                out=w1q[:, g, 512 * G:512 * G + 512].bitcast(FP8X4),
                scales=w1s[:, g, 512 * G:512 * G + 512],
                in_=w1g[(G, g)][:],
            )

        def period(i):
            n = i + 1
            tg = tpasses(n) if n < NCHUNK else []
            vg = [g for g in vpasses(n)] if n < NCHUNK else []
            if i >= 2:
                maxb(i - 2, 1)
            s1(i, 0)
            s1(i, 1)
            for g in vg:
                if g not in VSORT_ON_VECTOR:
                    vsort(n, g)
            hint(i - 1, 1)
            if i >= 2 and i % 2 == 1:
                diff(i - 2, 1)
            for g in tg[0:2]:
                sort(n, g)
            load_a(n + X_BUFS)
            qh(i - 1, 1)
            for g in tg[2:]:
                sort(n, g)
            load_b(n + X_BUFS)
            for g in vg:
                if g in VSORT_ON_VECTOR:
                    vsort(n, g)
            load_c(n + X_BUFS)
            for g in vg:
                vt(n, g)
            s1(i, 2)
            if i >= 2 and i % 2 == 1:
                sq(i - 2, 1)
            s1(i, 3)
            s2(i - 1, 0)
            maxb(i - 1, 0)
            for g in tg:
                trun(n, g)
            hint(i, 0)
            if i % 2 == 0:
                diff(i - 1, 0)
            for g in tg[0:1]:
                qx(n, g)
            qh(i, 0)
            for g in tg[1:]:
                qx(n, g)
            s1(i, 4)
            for g in vg[0:1]:
                vint(n, g)
                qx(n, g)
            s1(i, 5)
            for g in vg[1:]:
                vint(n, g)
                qx(n, g)
            if i % 2 == 0:
                sq(i - 1, 0)
            s1(i, 6)
            s1(i, 7)
            s2(i - 1, 1)

        load_a(0)
        w1_load(0, 0)
        w1_load(0, 1)
        load_b(0)
        w1_load(0, 2)
        w1_load(0, 3)
        for g in range(4):
            w1_load(1, g)
        for i in range(1, X_BUFS):
            load_a(i)
            load_b(i)
            load_c(i)

        psb = bank([P, 2, Z], 4)
        for r2 in range(2):
            nc.tensor.matmul(out=psb[:, r2, :], lhsT=negones[:], rhs=brow[:], start=True, stop=True)
        nc.vector.tensor_copy(out=nb2[:], in_=psb[:])
        nc.vector.tensor_copy(out=b1f[:], in_=b1t[:].rearrange("p g t -> p (g t)"))

        trun(0, 0, 0)
        trun(0, 1, 2)
        w1_copy(0, 0, 0)
        qx(0, 0)
        w1_quant(0, 0)
        qx(0, 1)
        w1_copy(0, 1, 1)
        head_open(0)
        head_pass(0, 0)
        trun(0, 2, 0)
        trun(0, 3, 2)
        w1_quant(0, 1)
        head_pass(0, 1)
        w1_copy(0, 2, 0)
        qx(0, 2)
        w1_quant(0, 2)
        head_pass(0, 2)
        w1_copy(0, 3, 1)
        qx(0, 3)
        w1_copy(1, 0, 0)
        w1_quant(0, 3)
        head_pass(0, 3)
        w1_copy(1, 1, 1)
        head_close(0)
        w2raw = work.tile([P, 2, 4, Z], BF16, name="w1raw", tag="w1raw", bufs=8)
        nc.sync.dma_start(out=w2raw[:], in_=W2.rearrange("(g p j) z -> p g j z", g=2, j=4))
        nc.sync.dma_start(out=qt[0:SUB, :], in_=q_energy.rearrange("a (b p) -> (a b) p", p=P))
        load_a(X_BUFS)
        load_b(X_BUFS)
        load_c(X_BUFS)

        w1_copy(1, 2, 0)
        w1_quant(1, 0)
        w1_quant(1, 1)
        head_open(1)
        head_pass(1, 0)
        head_pass(1, 1)
        w1_copy(1, 3, 0)
        w1_quant(1, 2)
        trun(1, 0, 0)
        trun(1, 1, 2)
        head_pass(1, 2)
        w1_quant(1, 3)
        qx(1, 0)
        qx(1, 1)
        trun(1, 2, 0)
        trun(1, 3, 2)
        load_a(1 + X_BUFS)
        load_b(1 + X_BUFS)
        load_c(1 + X_BUFS)
        head_pass(1, 3)
        head_close(1)
        qx(1, 2)
        qx(1, 3)
        hint(0, 0)
        w2g = work.tile([P, 2, Z, 4], BF16, name="w1g", tag="w1g", bufs=3, align_bytes=64)
        nc.vector.tensor_copy(out=w2g[:], in_=w2raw[:].rearrange("p g j z -> p g z j"))
        qh(0, 0)
        nc.vector.quantize_mx(out=w2q[:].bitcast(FP8X4), scales=w2s[:],
                              in_=w2g[:].rearrange("p g z j -> p (g z j)"))

        for i in range(1, NCHUNK):
            period(i)

        last = NCHUNK - 1
        maxb(last - 1, 1)
        hint(last, 1, 0, 256)
        hint(last, 1, 256, 512)
        qh(last, 1, 0, 256)
        qh(last, 1, 256, 512)
        s2(last, 0)
        s2(last, 1)
        maxb(last, 0)
        maxb(last, 1)
        diff(last, 0)
        diff(last, 1)
        sq(last, 0)
        sq(last, 1)

        rT = bank([P, P])
        nc.tensor.transpose(rT[:], res[:], ident[:])
        o = keep.tile([P, P], F32, name="o", tag="o")
        nc.vector.tensor_tensor(out=o[:], in0=rT[:], in1=qt[:], op=ALU.mult)
        outv = out.rearrange("a (b p) -> (a b) p", p=P)
        nc.sync.dma_start(out=outv[0:32, :], in_=o[0:32, :])
        nc.sync.dma_start(out=outv[32:SUB, :], in_=o[32:SUB, :])
